import numpy as np
import ml_dtypes


def mxq(x, axis, fmt="e4m3"):
    dtype, down = {"e4m3": (ml_dtypes.float8_e4m3fn, 7), "e5m2": (ml_dtypes.float8_e5m2, 14)}[fmt]
    v = np.moveaxis(np.asarray(x, np.float32).astype(ml_dtypes.bfloat16).astype(np.float64), axis, -1)
    blocks = v.reshape(v.shape[:-1] + (-1, 32))
    amax = np.abs(blocks).max(-1, keepdims=True)
    byte = np.maximum(np.where(amax > 0, np.frexp(amax)[1] - 1 + 127, 0) - down, 1)
    scale = np.exp2(byte - 127.0)
    codes = (blocks / scale).astype(np.float32).astype(dtype).astype(np.float64)
    return np.moveaxis((codes * scale).reshape(v.shape), -1, axis)


WIDE = False


def mx_kscale(k):
    if not WIDE:
        return np.ones(k)
    levels = np.array([10, -10, 5, -5, 0])
    a = np.random.permutation(np.resize(levels, k // 512 * 4)).reshape(k // 512, 4)
    idx = np.arange(k)
    return np.exp2(a[idx // 512, idx % 128 // 32])


BF16 = ml_dtypes.bfloat16


def bf(x):
    return np.asarray(x, np.float32).astype(BF16)


def f64(x):
    return np.asarray(x).astype(np.float64)


B, V, QK, DK, HC, WC, HS, WS = 4, 512, 512, 512, 32, 32, 32, 16
LQ = HC * WC
EPS = 1e-5
QS = np.sqrt(2.0) / DK ** 0.25


def mvn(x):
    mean = x.mean(axis=2, keepdims=True)
    var = x.var(axis=2, ddof=1, keepdims=True) + EPS
    return (x - mean) / np.sqrt(var)


def setup_inputs():
    s = mx_kscale(QK)
    g = 2.0 ** np.random.uniform(-9.0, 1.0, QK) * np.minimum(s, 1.0) ** 3
    f = g / np.sqrt(g * g + EPS)
    mu = 0.5 * np.random.standard_normal(QK)
    return {"c_1x": bf((np.random.standard_normal((B, QK, HC, WC)) + mu[None, :, None, None]) * g[None, :, None, None]),
            "f_w": bf(np.random.standard_normal((DK, QK)) * QS / np.sqrt(QK) / f[None, :]),
            "f_b": bf(np.random.standard_normal(DK) * 0.1)}


def reference(c_1x, f_w, f_b):
    xn = mvn(f64(c_1x).reshape(B, QK, LQ))
    y = (mxq(f64(f_w), 1, "e4m3") @ mxq(xn, 1, "e4m3")) + f64(f_b)[None, :, None]
    return y.transpose(0, 2, 1)

@@ -1,0 +1,178 @@
+from contextlib import ExitStack
+
+import concourse.mybir as mybir
+from concourse.masks import make_identity
+
+BF16 = mybir.dt.bfloat16
+F32 = mybir.dt.float32
+U32 = mybir.dt.uint32
+U8 = mybir.dt.uint8
+FP8X4 = mybir.dt.float8_e4m3fn_x4
+ALU = mybir.AluOpType
+ACT = mybir.ActivationFunctionType
+
+P = 128
+PACK = 4
+BATCH = 4
+CHANNELS = P * PACK
+PIXELS = 1024
+OUT_CH = 512
+EPS = 1e-5
+HALF = PIXELS // 2
+HALVES = PIXELS // HALF
+M_TILE = P
+TILES_PER_HALF = HALF // M_TILE
+TILES_PER_STORE = 2
+RUN = 4
+SCALAR_COLS = 384
+
+FLOPS = 2 * BATCH * PIXELS * CHANNELS * OUT_CH
+
+
+def tile_adaattn_pa_kernel(tc, c_1x, f_w, f_b, out):
+    nc = tc.nc
+    with ExitStack() as stack:
+        const = stack.enter_context(tc.tile_pool(name="const", bufs=1))
+        stats = stack.enter_context(tc.tile_pool(name="stats", bufs=BATCH))
+        scratch = stack.enter_context(tc.tile_pool(name="scratch", bufs=3))
+        work = stack.enter_context(tc.tile_pool(name="work", bufs=2))
+        results = stack.enter_context(tc.tile_pool(name="results", bufs=6))
+        psum = stack.enter_context(tc.psum_pool(name="psum", bufs=8))
+        stack.enter_context(tc.manual_schedule())
+
+        x_all = [const.tile([P, PACK, PIXELS], BF16, name="x%d" % b) for b in range(BATCH)]
+        mean_all = [stats.tile([P, PACK], F32, name="mean%d" % b, tag="mean") for b in range(BATCH)]
+        ssd_all = [stats.tile([P, PACK], F32, name="ssd%d" % b, tag="ssd") for b in range(BATCH)]
+        rstd_all = [stats.tile([P, PACK], F32, name="rstd%d" % b, tag="rstd") for b in range(BATCH)]
+        xn_all = {}
+        packed = {}
+        banks = {}
+
+        def mean_of(b):
+            for t in range(PACK):
+                v_junk = scratch.tile([P, PIXELS], BF16)
+                nc.vector.tensor_scalar(
+                    out=v_junk[:], in0=x_all[b][:, t, :], scalar1=1.0 / PIXELS, scalar2=None,
+                    op0=ALU.mult, op1=ALU.add, accum_out=mean_all[b][:, t : t + 1],
+                )
+
+        def squares_of(b, channels):
+            for t in channels:
+                s_junk = scratch.tile([P, PIXELS], BF16)
+                nc.scalar.activation(
+                    out=s_junk[:], in_=x_all[b][:, t, :], func=ACT.Square, scale=-1.0,
+                    bias=mean_all[b][:, t : t + 1], accum_out=ssd_all[b][:, t : t + 1],
+                )
+
+        def rstd_of(b):
+            var = stats.tile([P, PACK], F32)
+            nc.gpsimd.tensor_scalar(
+                out=var[:], in0=ssd_all[b][:], scalar1=1.0 / (PIXELS - 1), scalar2=EPS,
+                op0=ALU.mult, op1=ALU.add,
+            )
+            nc.gpsimd.tensor_tensor(out=rstd_all[b][:], in0=var[:], in1=minus_half[:], op=ALU.pow)
+
+        def normalise(b):
+            xn = work.tile([P, PACK, PIXELS], BF16)
+            for t in range(PACK):
+                nc.vector.tensor_scalar(
+                    out=xn[:, t, :], in0=x_all[b][:, t, :], scalar1=mean_all[b][:, t : t + 1],
+                    scalar2=rstd_all[b][:, t : t + 1], op0=ALU.subtract, op1=ALU.mult,
+                )
+            xn_all[b] = xn
+            grouped = work.tile([P, PIXELS, PACK], BF16, align_bytes=64)
+            codes = work.tile([P, PIXELS], U32, align_bytes=64)
+            scales = work.tile([P, PIXELS], U8, align_bytes=64)
+            packed[b] = (grouped, codes, scales)
+
+        def regroup(copy, b, first, count):
+            cols = slice(first, first + count)
+            copy(
+                out=packed[b][0][:, cols, :].rearrange("q (c i) t -> q c t i", i=RUN),
+                in_=xn_all[b][:, :, cols].rearrange("q t (c i) -> q c t i", i=RUN),
+            )
+
+        def quantise_and_multiply(b, h):
+            grouped, codes, scales = packed[b]
+            cols = slice(h * HALF, (h + 1) * HALF)
+            nc.vector.quantize_mx(
+                out=codes[:, cols].bitcast(FP8X4), scales=scales[:, cols],
+                in_=grouped[:, cols, :].rearrange("q w t -> q (w t)"),
+            )
+            banks[(b, h)] = []
+            for m in range(TILES_PER_HALF):
+                m_cols = slice(h * HALF + m * M_TILE, h * HALF + (m + 1) * M_TILE)
+                acc = psum.tile([M_TILE, OUT_CH], F32, tag="bank")
+                nc.tensor.matmul_mx(
+                    out=acc[:], lhsT=codes[:, m_cols].bitcast(FP8X4), lhsT_scale=scales[:, m_cols],
+                    rhs=w_codes[:].bitcast(FP8X4), rhs_scale=w_scales[:], start=True, stop=True,
+                )
+                banks[(b, h)].append(acc)
+
+        def add_bias_and_store(b, h):
+            for s in range(TILES_PER_HALF // TILES_PER_STORE):
+                o_sb = results.tile([P, TILES_PER_STORE, OUT_CH], F32)
+                for m in range(TILES_PER_STORE):
+                    acc = banks[(b, h)][s * TILES_PER_STORE + m]
+                    nc.vector.tensor_tensor(out=o_sb[:, m, :], in0=acc[:], in1=bias[:], op=ALU.add)
+                first = h * HALF + s * TILES_PER_STORE * M_TILE
+                nc.sync.dma_start(
+                    out=out[b, first : first + TILES_PER_STORE * M_TILE, :].rearrange("(m p) o -> p m o", p=P),
+                    in_=o_sb[:],
+                )
+
+        minus_half = const.tile([P, PACK], F32)
+        nc.gpsimd.memset(minus_half[:], -0.5)
+        ident = const.tile([P, P], F32)
+        make_identity(nc, ident[:])
+        bias = const.tile([P, OUT_CH], BF16)
+        nc.scalar.dma_start(out=bias[:], in_=f_b.partition_broadcast(P))
+        x_dram = [c_1x[b].rearrange("(q t) h w -> q t (h w)", t=PACK) for b in range(BATCH)]
+        w_sb = const.tile([P, OUT_CH // P, CHANNELS], BF16)
+        for t in range(PACK):
+            nc.sync.dma_start(out=x_all[0][:, t, :], in_=x_dram[0][:, t, :])
+        nc.sync.dma_start(out=w_sb[:], in_=f_w.rearrange("(a o) c -> o a c", o=P))
+        for b in range(1, BATCH):
+            nc.sync.dma_start(out=x_all[b][:], in_=x_dram[b])
+
+        mean_of(0)
+        squares_of(0, range(PACK))
+        rstd_of(0)
+
+        w_words = w_sb[:].bitcast(F32).rearrange("o a (q u) -> o a u q", u=2)
+        w_grouped = const.tile([P, OUT_CH * PACK], BF16, align_bytes=64)
+        w_grouped_words = w_grouped[:].bitcast(F32).rearrange("q (a o u) -> q a o u", o=P, u=2)
+        for pair in range(2):
+            w_t = psum.tile([P, 2, 2, P], F32, tag="bank")
+            for a in range(2):
+                for u in range(2):
+                    nc.tensor.transpose(w_t[:, a, u, :], w_words[:, 2 * pair + a, u, :], ident[:])
+            nc.vector.tensor_copy(
+                out=w_grouped_words[:, 2 * pair : 2 * pair + 2, :, :],
+                in_=w_t[:].rearrange("q a u o -> q a o u"),
+            )
+        w_codes = const.tile([P, OUT_CH], U32, align_bytes=64)
+        w_scales = const.tile([P, OUT_CH], U8, align_bytes=64)
+        nc.vector.quantize_mx(out=w_codes[:].bitcast(FP8X4), scales=w_scales[:], in_=w_grouped[:])
+
+        mean_of(1)
+        normalise(0)
+        mean_of(2)
+        mean_of(3)
+
+        waiting = None
+        for b in range(BATCH):
+            for h in range(HALVES):
+                if b + 1 < BATCH:
+                    squares_of(b + 1, range(2 * h, 2 * h + 2))
+                    if h == HALVES - 1:
+                        rstd_of(b + 1)
+                regroup(nc.scalar.copy, b, h * HALF, SCALAR_COLS)
+                regroup(nc.vector.tensor_copy, b, h * HALF + SCALAR_COLS, HALF - SCALAR_COLS)
+                if b + 1 < BATCH and h == HALVES - 1:
+                    normalise(b + 1)
+                quantise_and_multiply(b, h)
+                if waiting is not None:
+                    add_bias_and_store(waiting[0], waiting[1])
+                waiting = (b, h)
+        add_bias_and_store(waiting[0], waiting[1])

@@ -22,7 +22,6 @@ HALF = PIXELS // 2
 HALVES = PIXELS // HALF
 M_TILE = P
 TILES_PER_HALF = HALF // M_TILE
-TILES_PER_STORE = 2
 RUN = 4
 SCALAR_COLS = 384
 
@@ -36,7 +35,7 @@ def tile_adaattn_pa_kernel(tc, c_1x, f_w, f_b, out):
         stats = stack.enter_context(tc.tile_pool(name="stats", bufs=BATCH))
         scratch = stack.enter_context(tc.tile_pool(name="scratch", bufs=3))
         work = stack.enter_context(tc.tile_pool(name="work", bufs=2))
-        results = stack.enter_context(tc.tile_pool(name="results", bufs=6))
+        results = stack.enter_context(tc.tile_pool(name="results", bufs=8))
         psum = stack.enter_context(tc.psum_pool(name="psum", bufs=8))
         stack.enter_context(tc.manual_schedule())
 
@@ -56,15 +55,13 @@ def tile_adaattn_pa_kernel(tc, c_1x, f_w, f_b, out):
                     op0=ALU.mult, op1=ALU.add, accum_out=mean_all[b][:, t : t + 1],
                 )
 
-        def squares_of(b, channels):
-            for t in channels:
+        def rstd_of(b):
+            for t in range(PACK):
                 s_junk = scratch.tile([P, PIXELS], BF16)
                 nc.scalar.activation(
                     out=s_junk[:], in_=x_all[b][:, t, :], func=ACT.Square, scale=-1.0,
                     bias=mean_all[b][:, t : t + 1], accum_out=ssd_all[b][:, t : t + 1],
                 )
-
-        def rstd_of(b):
             var = stats.tile([P, PACK], F32)
             nc.gpsimd.tensor_scalar(
                 out=var[:], in0=ssd_all[b][:], scalar1=1.0 / (PIXELS - 1), scalar2=EPS,
@@ -93,6 +90,8 @@ def tile_adaattn_pa_kernel(tc, c_1x, f_w, f_b, out):
             )
 
         def quantise_and_multiply(b, h):
+            regroup(nc.scalar.copy, b, h * HALF, SCALAR_COLS)
+            regroup(nc.vector.tensor_copy, b, h * HALF + SCALAR_COLS, HALF - SCALAR_COLS)
             grouped, codes, scales = packed[b]
             cols = slice(h * HALF, (h + 1) * HALF)
             nc.vector.quantize_mx(
@@ -110,33 +109,28 @@ def tile_adaattn_pa_kernel(tc, c_1x, f_w, f_b, out):
                 banks[(b, h)].append(acc)
 
         def add_bias_and_store(b, h):
-            for s in range(TILES_PER_HALF // TILES_PER_STORE):
-                o_sb = results.tile([P, TILES_PER_STORE, OUT_CH], F32)
-                for m in range(TILES_PER_STORE):
-                    acc = banks[(b, h)][s * TILES_PER_STORE + m]
-                    nc.vector.tensor_tensor(out=o_sb[:, m, :], in0=acc[:], in1=bias[:], op=ALU.add)
-                first = h * HALF + s * TILES_PER_STORE * M_TILE
-                nc.sync.dma_start(
-                    out=out[b, first : first + TILES_PER_STORE * M_TILE, :].rearrange("(m p) o -> p m o", p=P),
-                    in_=o_sb[:],
-                )
+            for m in range(TILES_PER_HALF):
+                o_sb = results.tile([M_TILE, OUT_CH], F32)
+                nc.vector.tensor_tensor(out=o_sb[:], in0=banks[(b, h)][m][:], in1=bias[:], op=ALU.add)
+                first = h * HALF + m * M_TILE
+                nc.sync.dma_start(out=out[b, first : first + M_TILE, :], in_=o_sb[:])
 
         minus_half = const.tile([P, PACK], F32)
         nc.gpsimd.memset(minus_half[:], -0.5)
         ident = const.tile([P, P], F32)
         make_identity(nc, ident[:])
-        bias = const.tile([P, OUT_CH], BF16)
-        nc.scalar.dma_start(out=bias[:], in_=f_b.partition_broadcast(P))
         x_dram = [c_1x[b].rearrange("(q t) h w -> q t (h w)", t=PACK) for b in range(BATCH)]
         w_sb = const.tile([P, OUT_CH // P, CHANNELS], BF16)
+        bias = const.tile([P, OUT_CH], BF16)
         for t in range(PACK):
             nc.sync.dma_start(out=x_all[0][:, t, :], in_=x_dram[0][:, t, :])
         nc.sync.dma_start(out=w_sb[:], in_=f_w.rearrange("(a o) c -> o a c", o=P))
-        for b in range(1, BATCH):
-            nc.sync.dma_start(out=x_all[b][:], in_=x_dram[b])
+        nc.sync.dma_start(out=x_all[1][:], in_=x_dram[1])
+        nc.sync.dma_start(out=bias[:], in_=f_b.partition_broadcast(P))
+        nc.sync.dma_start(out=x_all[2][:], in_=x_dram[2])
+        nc.sync.dma_start(out=x_all[3][:], in_=x_dram[3])
 
         mean_of(0)
-        squares_of(0, range(PACK))
         rstd_of(0)
 
         w_words = w_sb[:].bitcast(F32).rearrange("o a (q u) -> o a u q", u=2)
@@ -147,15 +141,16 @@ def tile_adaattn_pa_kernel(tc, c_1x, f_w, f_b, out):
             for a in range(2):
                 for u in range(2):
                     nc.tensor.transpose(w_t[:, a, u, :], w_words[:, 2 * pair + a, u, :], ident[:])
-            nc.vector.tensor_copy(
+            nc.scalar.copy(
                 out=w_grouped_words[:, 2 * pair : 2 * pair + 2, :, :],
                 in_=w_t[:].rearrange("q a u o -> q a o u"),
             )
         w_codes = const.tile([P, OUT_CH], U32, align_bytes=64)
         w_scales = const.tile([P, OUT_CH], U8, align_bytes=64)
-        nc.vector.quantize_mx(out=w_codes[:].bitcast(FP8X4), scales=w_scales[:], in_=w_grouped[:])
 
         mean_of(1)
+        rstd_of(1)
+        nc.vector.quantize_mx(out=w_codes[:].bitcast(FP8X4), scales=w_scales[:], in_=w_grouped[:])
         normalise(0)
         mean_of(2)
         mean_of(3)
@@ -163,15 +158,12 @@ def tile_adaattn_pa_kernel(tc, c_1x, f_w, f_b, out):
         waiting = None
         for b in range(BATCH):
             for h in range(HALVES):
-                if b + 1 < BATCH:
-                    squares_of(b + 1, range(2 * h, 2 * h + 2))
-                    if h == HALVES - 1:
-                        rstd_of(b + 1)
-                regroup(nc.scalar.copy, b, h * HALF, SCALAR_COLS)
-                regroup(nc.vector.tensor_copy, b, h * HALF + SCALAR_COLS, HALF - SCALAR_COLS)
-                if b + 1 < BATCH and h == HALVES - 1:
-                    normalise(b + 1)
                 quantise_and_multiply(b, h)
+                if h == HALVES - 1:
+                    if b + 2 < BATCH:
+                        rstd_of(b + 2)
+                    if b + 1 < BATCH:
+                        normalise(b + 1)
                 if waiting is not None:
                     add_bias_and_store(waiting[0], waiting[1])
                 waiting = (b, h)

@@ -109,11 +109,15 @@ def tile_adaattn_pa_kernel(tc, c_1x, f_w, f_b, out):
                 banks[(b, h)].append(acc)
 
         def add_bias_and_store(b, h):
-            for m in range(TILES_PER_HALF):
+            o_first = results.tile([M_TILE, OUT_CH], F32)
+            nc.scalar.copy(out=o_first[:], in_=banks[(b, h)][0][:])
+            nc.gpsimd.tensor_tensor(out=o_first[:], in0=o_first[:], in1=bias[:], op=ALU.add)
+            for m in range(1, TILES_PER_HALF):
                 o_sb = results.tile([M_TILE, OUT_CH], F32)
                 nc.vector.tensor_tensor(out=o_sb[:], in0=banks[(b, h)][m][:], in1=bias[:], op=ALU.add)
                 first = h * HALF + m * M_TILE
                 nc.sync.dma_start(out=out[b, first : first + M_TILE, :], in_=o_sb[:])
+            nc.sync.dma_start(out=out[b, h * HALF : h * HALF + M_TILE, :], in_=o_first[:])
 
         minus_half = const.tile([P, PACK], F32)
         nc.gpsimd.memset(minus_half[:], -0.5)

@@ -23,7 +23,7 @@ HALVES = PIXELS // HALF
 M_TILE = P
 TILES_PER_HALF = HALF // M_TILE
 RUN = 4
-SCALAR_COLS = 384
+VECTOR_COLS = 128
 
 FLOPS = 2 * BATCH * PIXELS * CHANNELS * OUT_CH
 
@@ -89,9 +89,15 @@ def tile_adaattn_pa_kernel(tc, c_1x, f_w, f_b, out):
                 in_=xn_all[b][:, :, cols].rearrange("q t (c i) -> q c t i", i=RUN),
             )
 
+        def vector_cols(b):
+            return VECTOR_COLS if b + 2 < BATCH else 0
+
+        def regroup_on_vector(b, h):
+            if vector_cols(b) > 0:
+                regroup(nc.vector.tensor_copy, b, (h + 1) * HALF - vector_cols(b), vector_cols(b))
+
         def quantise_and_multiply(b, h):
-            regroup(nc.scalar.copy, b, h * HALF, SCALAR_COLS)
-            regroup(nc.vector.tensor_copy, b, h * HALF + SCALAR_COLS, HALF - SCALAR_COLS)
+            regroup(nc.scalar.copy, b, h * HALF, HALF - vector_cols(b))
             grouped, codes, scales = packed[b]
             cols = slice(h * HALF, (h + 1) * HALF)
             nc.vector.quantize_mx(
@@ -108,16 +114,12 @@ def tile_adaattn_pa_kernel(tc, c_1x, f_w, f_b, out):
                 )
                 banks[(b, h)].append(acc)
 
-        def add_bias_and_store(b, h):
-            o_first = results.tile([M_TILE, OUT_CH], F32)
-            nc.scalar.copy(out=o_first[:], in_=banks[(b, h)][0][:])
-            nc.gpsimd.tensor_tensor(out=o_first[:], in0=o_first[:], in1=bias[:], op=ALU.add)
-            for m in range(1, TILES_PER_HALF):
+        def add_bias_and_store(b, h, tiles):
+            for m in tiles:
                 o_sb = results.tile([M_TILE, OUT_CH], F32)
                 nc.vector.tensor_tensor(out=o_sb[:], in0=banks[(b, h)][m][:], in1=bias[:], op=ALU.add)
                 first = h * HALF + m * M_TILE
                 nc.sync.dma_start(out=out[b, first : first + M_TILE, :], in_=o_sb[:])
-            nc.sync.dma_start(out=out[b, h * HALF : h * HALF + M_TILE, :], in_=o_first[:])
 
         minus_half = const.tile([P, PACK], F32)
         nc.gpsimd.memset(minus_half[:], -0.5)
@@ -130,8 +132,8 @@ def tile_adaattn_pa_kernel(tc, c_1x, f_w, f_b, out):
             nc.sync.dma_start(out=x_all[0][:, t, :], in_=x_dram[0][:, t, :])
         nc.sync.dma_start(out=w_sb[:], in_=f_w.rearrange("(a o) c -> o a c", o=P))
         nc.sync.dma_start(out=x_all[1][:], in_=x_dram[1])
-        nc.sync.dma_start(out=bias[:], in_=f_b.partition_broadcast(P))
         nc.sync.dma_start(out=x_all[2][:], in_=x_dram[2])
+        nc.sync.dma_start(out=bias[:], in_=f_b.partition_broadcast(P))
         nc.sync.dma_start(out=x_all[3][:], in_=x_dram[3])
 
         mean_of(0)
@@ -145,7 +147,7 @@ def tile_adaattn_pa_kernel(tc, c_1x, f_w, f_b, out):
             for a in range(2):
                 for u in range(2):
                     nc.tensor.transpose(w_t[:, a, u, :], w_words[:, 2 * pair + a, u, :], ident[:])
-            nc.scalar.copy(
+            nc.vector.tensor_copy(
                 out=w_grouped_words[:, 2 * pair : 2 * pair + 2, :, :],
                 in_=w_t[:].rearrange("q a u o -> q a o u"),
             )
@@ -157,18 +159,28 @@ def tile_adaattn_pa_kernel(tc, c_1x, f_w, f_b, out):
         nc.vector.quantize_mx(out=w_codes[:].bitcast(FP8X4), scales=w_scales[:], in_=w_grouped[:])
         normalise(0)
         mean_of(2)
-        mean_of(3)
+        regroup_on_vector(0, 0)
 
+        early = range(TILES_PER_HALF // 2)
+        late = range(TILES_PER_HALF // 2, TILES_PER_HALF)
         waiting = None
         for b in range(BATCH):
             for h in range(HALVES):
+                if h == HALVES - 1 and b + 1 < BATCH:
+                    normalise(b + 1)
+                if waiting is not None:
+                    add_bias_and_store(waiting[0], waiting[1], early)
                 quantise_and_multiply(b, h)
                 if h == HALVES - 1:
                     if b + 2 < BATCH:
                         rstd_of(b + 2)
+                    if b + 3 < BATCH:
+                        mean_of(b + 3)
                     if b + 1 < BATCH:
-                        normalise(b + 1)
+                        regroup_on_vector(b + 1, 0)
+                else:
+                    regroup_on_vector(b, h + 1)
                 if waiting is not None:
-                    add_bias_and_store(waiting[0], waiting[1])
+                    add_bias_and_store(waiting[0], waiting[1], late)
                 waiting = (b, h)
-        add_bias_and_store(waiting[0], waiting[1])
+        add_bias_and_store(waiting[0], waiting[1], range(TILES_PER_HALF))

@@ -123,6 +123,8 @@ def tile_adaattn_pa_kernel(tc, c_1x, f_w, f_b, out):
 
         minus_half = const.tile([P, PACK], F32)
         nc.gpsimd.memset(minus_half[:], -0.5)
+        table_junk = const.tile([P, 1], F32)
+        nc.scalar.activation(out=table_junk[:], in_=minus_half[:, 0:1], func=ACT.Square)
         ident = const.tile([P, P], F32)
         make_identity(nc, ident[:])
         x_dram = [c_1x[b].rearrange("(q t) h w -> q t (h w)", t=PACK) for b in range(BATCH)]

@@ -132,14 +132,17 @@ def tile_adaattn_pa_kernel(tc, c_1x, f_w, f_b, out):
         bias = const.tile([P, OUT_CH], BF16)
         for t in range(PACK):
             nc.sync.dma_start(out=x_all[0][:, t, :], in_=x_dram[0][:, t, :])
+        for t in range(PACK):
+            nc.sync.dma_start(out=x_all[1][:, t, :], in_=x_dram[1][:, t, :])
         nc.sync.dma_start(out=w_sb[:], in_=f_w.rearrange("(a o) c -> o a c", o=P))
-        nc.sync.dma_start(out=x_all[1][:], in_=x_dram[1])
         nc.sync.dma_start(out=x_all[2][:], in_=x_dram[2])
         nc.sync.dma_start(out=bias[:], in_=f_b.partition_broadcast(P))
         nc.sync.dma_start(out=x_all[3][:], in_=x_dram[3])
 
         mean_of(0)
         rstd_of(0)
+        mean_of(1)
+        rstd_of(1)
 
         w_words = w_sb[:].bitcast(F32).rearrange("o a (q u) -> o a u q", u=2)
         w_grouped = const.tile([P, OUT_CH * PACK], BF16, align_bytes=64)
@@ -156,8 +159,6 @@ def tile_adaattn_pa_kernel(tc, c_1x, f_w, f_b, out):
         w_codes = const.tile([P, OUT_CH], U32, align_bytes=64)
         w_scales = const.tile([P, OUT_CH], U8, align_bytes=64)
 
-        mean_of(1)
-        rstd_of(1)
         nc.vector.quantize_mx(out=w_codes[:].bitcast(FP8X4), scales=w_scales[:], in_=w_grouped[:])
         normalise(0)
         mean_of(2)

@@ -60,13 +60,26 @@ def tile_adaattn_pa_kernel(tc, c_1x, f_w, f_b, out):
                 s_junk = scratch.tile([P, PIXELS], BF16)
                 nc.scalar.activation(
                     out=s_junk[:], in_=x_all[b][:, t, :], func=ACT.Square, scale=-1.0,
-                    bias=mean_all[b][:, t : t + 1], accum_out=ssd_all[b][:, t : t + 1],
+                    bias=x_all[b][:, t, 0:1], accum_out=ssd_all[b][:, t : t + 1],
                 )
-            var = stats.tile([P, PACK], F32)
+            shift = stats.tile([P, PACK], F32)
+            nc.gpsimd.tensor_tensor(
+                out=shift[:], in0=mean_all[b][:], in1=x_all[b][:, :, 0], op=ALU.subtract
+            )
+            shift_sq = stats.tile([P, PACK], F32)
+            nc.gpsimd.tensor_tensor(out=shift_sq[:], in0=shift[:], in1=shift[:], op=ALU.mult)
+            offset = stats.tile([P, PACK], F32)
             nc.gpsimd.tensor_scalar(
-                out=var[:], in0=ssd_all[b][:], scalar1=1.0 / (PIXELS - 1), scalar2=EPS,
+                out=offset[:], in0=shift_sq[:], scalar1=-PIXELS / (PIXELS - 1), scalar2=EPS,
                 op0=ALU.mult, op1=ALU.add,
             )
+            scaled = stats.tile([P, PACK], F32)
+            nc.gpsimd.tensor_scalar(
+                out=scaled[:], in0=ssd_all[b][:], scalar1=1.0 / (PIXELS - 1), scalar2=0.0,
+                op0=ALU.mult, op1=ALU.add,
+            )
+            var = stats.tile([P, PACK], F32)
+            nc.gpsimd.tensor_tensor(out=var[:], in0=scaled[:], in1=offset[:], op=ALU.add)
             nc.gpsimd.tensor_tensor(out=rstd_all[b][:], in0=var[:], in1=minus_half[:], op=ALU.pow)
 
         def normalise(b):
@@ -143,6 +156,7 @@ def tile_adaattn_pa_kernel(tc, c_1x, f_w, f_b, out):
         rstd_of(0)
         mean_of(1)
         rstd_of(1)
+        normalise(0)
 
         w_words = w_sb[:].bitcast(F32).rearrange("o a (q u) -> o a u q", u=2)
         w_grouped = const.tile([P, OUT_CH * PACK], BF16, align_bytes=64)
@@ -160,7 +174,6 @@ def tile_adaattn_pa_kernel(tc, c_1x, f_w, f_b, out):
         w_scales = const.tile([P, OUT_CH], U8, align_bytes=64)
 
         nc.vector.quantize_mx(out=w_codes[:].bitcast(FP8X4), scales=w_scales[:], in_=w_grouped[:])
-        normalise(0)
         mean_of(2)
         regroup_on_vector(0, 0)
 

@@ -10,6 +10,7 @@ U8 = mybir.dt.uint8
 FP8X4 = mybir.dt.float8_e4m3fn_x4
 ALU = mybir.AluOpType
 ACT = mybir.ActivationFunctionType
+AXIS = mybir.AxisListType
 
 P = 128
 PACK = 4
@@ -23,7 +24,9 @@ HALVES = PIXELS // HALF
 M_TILE = P
 TILES_PER_HALF = HALF // M_TILE
 RUN = 4
-VECTOR_COLS = 128
+VECTOR_COLS = (256, 128, 0, 0)
+SUMMED = {2: (2, 3), 3: (0, 1, 2, 3)}
+CHUNKS = PIXELS // P
 
 FLOPS = 2 * BATCH * PIXELS * CHANNELS * OUT_CH
 
@@ -36,7 +39,8 @@ def tile_adaattn_pa_kernel(tc, c_1x, f_w, f_b, out):
         scratch = stack.enter_context(tc.tile_pool(name="scratch", bufs=3))
         work = stack.enter_context(tc.tile_pool(name="work", bufs=2))
         results = stack.enter_context(tc.tile_pool(name="results", bufs=8))
-        psum = stack.enter_context(tc.psum_pool(name="psum", bufs=8))
+        psum = stack.enter_context(tc.psum_pool(name="psum", bufs=7))
+        psum_sums = stack.enter_context(tc.psum_pool(name="psum_sums", bufs=1))
         stack.enter_context(tc.manual_schedule())
 
         x_all = [const.tile([P, PACK, PIXELS], BF16, name="x%d" % b) for b in range(BATCH)]
@@ -46,22 +50,44 @@ def tile_adaattn_pa_kernel(tc, c_1x, f_w, f_b, out):
         xn_all = {}
         packed = {}
         banks = {}
+        sums_all = {}
 
         def mean_of(b):
             for t in range(PACK):
+                if t in SUMMED.get(b, ()):
+                    continue
                 v_junk = scratch.tile([P, PIXELS], BF16)
                 nc.vector.tensor_scalar(
                     out=v_junk[:], in0=x_all[b][:, t, :], scalar1=1.0 / PIXELS, scalar2=None,
                     op0=ALU.mult, op1=ALU.add, accum_out=mean_all[b][:, t : t + 1],
                 )
 
-        def rstd_of(b):
+        def partial_sums(b, slots):
+            if b not in sums_all:
+                sums_all[b] = psum_sums.tile([P, PACK, P], F32, name="sums%d" % b, tag="sums")
+            for t in slots:
+                for chunk in range(CHUNKS):
+                    nc.tensor.matmul(
+                        sums_all[b][:, t, :], lhsT=ident_mean[:],
+                        rhs=x_all[b][:, t, chunk * P : (chunk + 1) * P],
+                        start=chunk == 0, stop=chunk == CHUNKS - 1,
+                    )
+
+        def mean_from_sums(b):
+            slots = slice(SUMMED[b][0], SUMMED[b][-1] + 1)
+            nc.vector.tensor_reduce(
+                out=mean_all[b][:, slots], in_=sums_all[b][:, slots, :], op=ALU.add, axis=AXIS.X
+            )
+
+        def squares_of(b):
             for t in range(PACK):
                 s_junk = scratch.tile([P, PIXELS], BF16)
                 nc.scalar.activation(
                     out=s_junk[:], in_=x_all[b][:, t, :], func=ACT.Square, scale=-1.0,
                     bias=x_all[b][:, t, 0:1], accum_out=ssd_all[b][:, t : t + 1],
                 )
+
+        def rstd_of(b):
             shift = stats.tile([P, PACK], F32)
             nc.gpsimd.tensor_tensor(
                 out=shift[:], in0=mean_all[b][:], in1=x_all[b][:, :, 0], op=ALU.subtract
@@ -102,15 +128,12 @@ def tile_adaattn_pa_kernel(tc, c_1x, f_w, f_b, out):
                 in_=xn_all[b][:, :, cols].rearrange("q t (c i) -> q c t i", i=RUN),
             )
 
-        def vector_cols(b):
-            return VECTOR_COLS if b + 2 < BATCH else 0
-
         def regroup_on_vector(b, h):
-            if vector_cols(b) > 0:
-                regroup(nc.vector.tensor_copy, b, (h + 1) * HALF - vector_cols(b), vector_cols(b))
+            if VECTOR_COLS[b] > 0:
+                regroup(nc.vector.tensor_copy, b, (h + 1) * HALF - VECTOR_COLS[b], VECTOR_COLS[b])
 
         def quantise_and_multiply(b, h):
-            regroup(nc.scalar.copy, b, h * HALF, HALF - vector_cols(b))
+            regroup(nc.scalar.copy, b, h * HALF, HALF - VECTOR_COLS[b])
             grouped, codes, scales = packed[b]
             cols = slice(h * HALF, (h + 1) * HALF)
             nc.vector.quantize_mx(
@@ -140,23 +163,30 @@ def tile_adaattn_pa_kernel(tc, c_1x, f_w, f_b, out):
         nc.scalar.activation(out=table_junk[:], in_=minus_half[:, 0:1], func=ACT.Square)
         ident = const.tile([P, P], F32)
         make_identity(nc, ident[:])
+        ident_mean = const.tile([P, P], BF16)
+        nc.gpsimd.tensor_scalar(
+            out=ident_mean[:], in0=ident[:], scalar1=1.0 / PIXELS, scalar2=0.0,
+            op0=ALU.mult, op1=ALU.add,
+        )
         x_dram = [c_1x[b].rearrange("(q t) h w -> q t (h w)", t=PACK) for b in range(BATCH)]
         w_sb = const.tile([P, OUT_CH // P, CHANNELS], BF16)
         bias = const.tile([P, OUT_CH], BF16)
         for t in range(PACK):
             nc.sync.dma_start(out=x_all[0][:, t, :], in_=x_dram[0][:, t, :])
         for t in range(PACK):
+            if t == PACK // 2:
+                nc.sync.dma_start(out=w_sb[:], in_=f_w.rearrange("(a o) c -> o a c", o=P))
             nc.sync.dma_start(out=x_all[1][:, t, :], in_=x_dram[1][:, t, :])
-        nc.sync.dma_start(out=w_sb[:], in_=f_w.rearrange("(a o) c -> o a c", o=P))
         nc.sync.dma_start(out=x_all[2][:], in_=x_dram[2])
         nc.sync.dma_start(out=bias[:], in_=f_b.partition_broadcast(P))
         nc.sync.dma_start(out=x_all[3][:], in_=x_dram[3])
 
         mean_of(0)
+        squares_of(0)
         rstd_of(0)
         mean_of(1)
+        squares_of(1)
         rstd_of(1)
-        normalise(0)
 
         w_words = w_sb[:].bitcast(F32).rearrange("o a (q u) -> o a u q", u=2)
         w_grouped = const.tile([P, OUT_CH * PACK], BF16, align_bytes=64)
@@ -173,30 +203,40 @@ def tile_adaattn_pa_kernel(tc, c_1x, f_w, f_b, out):
         w_codes = const.tile([P, OUT_CH], U32, align_bytes=64)
         w_scales = const.tile([P, OUT_CH], U8, align_bytes=64)
 
+        normalise(0)
         nc.vector.quantize_mx(out=w_codes[:].bitcast(FP8X4), scales=w_scales[:], in_=w_grouped[:])
+        partial_sums(2, SUMMED[2])
         mean_of(2)
         regroup_on_vector(0, 0)
 
         early = range(TILES_PER_HALF // 2)
         late = range(TILES_PER_HALF // 2, TILES_PER_HALF)
         waiting = None
+        sums_after = [SUMMED[3][:2], SUMMED[3][2:3], SUMMED[3][3:]]
         for b in range(BATCH):
             for h in range(HALVES):
+                step = b * HALVES + h
                 if h == HALVES - 1 and b + 1 < BATCH:
                     normalise(b + 1)
                 if waiting is not None:
                     add_bias_and_store(waiting[0], waiting[1], early)
                 quantise_and_multiply(b, h)
+                if step < len(sums_after):
+                    partial_sums(3, sums_after[step])
+                if step == 0:
+                    mean_from_sums(2)
                 if h == HALVES - 1:
                     if b + 2 < BATCH:
-                        rstd_of(b + 2)
-                    if b + 3 < BATCH:
-                        mean_of(b + 3)
+                        squares_of(b + 2)
                     if b + 1 < BATCH:
                         regroup_on_vector(b + 1, 0)
                 else:
                     regroup_on_vector(b, h + 1)
                 if waiting is not None:
                     add_bias_and_store(waiting[0], waiting[1], late)
+                if step == len(sums_after):
+                    mean_from_sums(3)
+                if h == HALVES - 1 and b + 2 < BATCH:
+                    rstd_of(b + 2)
                 waiting = (b, h)
         add_bias_and_store(waiting[0], waiting[1], range(TILES_PER_HALF))

@@ -79,8 +79,8 @@ def tile_adaattn_pa_kernel(tc, c_1x, f_w, f_b, out):
                 out=mean_all[b][:, slots], in_=sums_all[b][:, slots, :], op=ALU.add, axis=AXIS.X
             )
 
-        def squares_of(b):
-            for t in range(PACK):
+        def squares_of(b, slots):
+            for t in slots:
                 s_junk = scratch.tile([P, PIXELS], BF16)
                 nc.scalar.activation(
                     out=s_junk[:], in_=x_all[b][:, t, :], func=ACT.Square, scale=-1.0,
@@ -94,9 +94,9 @@ def tile_adaattn_pa_kernel(tc, c_1x, f_w, f_b, out):
             )
             shift_sq = stats.tile([P, PACK], F32)
             nc.gpsimd.tensor_tensor(out=shift_sq[:], in0=shift[:], in1=shift[:], op=ALU.mult)
-            offset = stats.tile([P, PACK], F32)
+            correction = stats.tile([P, PACK], F32)
             nc.gpsimd.tensor_scalar(
-                out=offset[:], in0=shift_sq[:], scalar1=-PIXELS / (PIXELS - 1), scalar2=EPS,
+                out=correction[:], in0=shift_sq[:], scalar1=-PIXELS / (PIXELS - 1), scalar2=EPS,
                 op0=ALU.mult, op1=ALU.add,
             )
             scaled = stats.tile([P, PACK], F32)
@@ -105,7 +105,7 @@ def tile_adaattn_pa_kernel(tc, c_1x, f_w, f_b, out):
                 op0=ALU.mult, op1=ALU.add,
             )
             var = stats.tile([P, PACK], F32)
-            nc.gpsimd.tensor_tensor(out=var[:], in0=scaled[:], in1=offset[:], op=ALU.add)
+            nc.gpsimd.tensor_tensor(out=var[:], in0=scaled[:], in1=correction[:], op=ALU.add)
             nc.gpsimd.tensor_tensor(out=rstd_all[b][:], in0=var[:], in1=minus_half[:], op=ALU.pow)
 
         def normalise(b):
@@ -182,10 +182,10 @@ def tile_adaattn_pa_kernel(tc, c_1x, f_w, f_b, out):
         nc.sync.dma_start(out=x_all[3][:], in_=x_dram[3])
 
         mean_of(0)
-        squares_of(0)
+        squares_of(0, range(PACK))
         rstd_of(0)
         mean_of(1)
-        squares_of(1)
+        squares_of(1, range(PACK))
         rstd_of(1)
 
         w_words = w_sb[:].bitcast(F32).rearrange("o a (q u) -> o a u q", u=2)
@@ -213,21 +213,22 @@ def tile_adaattn_pa_kernel(tc, c_1x, f_w, f_b, out):
         late = range(TILES_PER_HALF // 2, TILES_PER_HALF)
         waiting = None
         sums_after = [SUMMED[3][:2], SUMMED[3][2:3], SUMMED[3][3:]]
+        squares_after = {1: (2, (0, 1, 2, 3)), 3: (3, (0, 1, 2)), 4: (3, (3,))}
         for b in range(BATCH):
             for h in range(HALVES):
                 step = b * HALVES + h
-                if h == HALVES - 1 and b + 1 < BATCH:
-                    normalise(b + 1)
                 if waiting is not None:
                     add_bias_and_store(waiting[0], waiting[1], early)
+                if h == HALVES - 1 and b + 1 < BATCH:
+                    normalise(b + 1)
                 quantise_and_multiply(b, h)
                 if step < len(sums_after):
                     partial_sums(3, sums_after[step])
                 if step == 0:
                     mean_from_sums(2)
+                if step in squares_after:
+                    squares_of(*squares_after[step])
                 if h == HALVES - 1:
-                    if b + 2 < BATCH:
-                        squares_of(b + 2)
                     if b + 1 < BATCH:
                         regroup_on_vector(b + 1, 0)
                 else:
@@ -236,7 +237,7 @@ def tile_adaattn_pa_kernel(tc, c_1x, f_w, f_b, out):
                     add_bias_and_store(waiting[0], waiting[1], late)
                 if step == len(sums_after):
                     mean_from_sums(3)
-                if h == HALVES - 1 and b + 2 < BATCH:
-                    rstd_of(b + 2)
+                if step in squares_after and squares_after[step][1][-1] == PACK - 1:
+                    rstd_of(squares_after[step][0])
                 waiting = (b, h)
         add_bias_and_store(waiting[0], waiting[1], range(TILES_PER_HALF))

@@ -46,11 +46,13 @@ def tile_adaattn_pa_kernel(tc, c_1x, f_w, f_b, out):
         x_all = [const.tile([P, PACK, PIXELS], BF16, name="x%d" % b) for b in range(BATCH)]
         mean_all = [stats.tile([P, PACK], F32, name="mean%d" % b, tag="mean") for b in range(BATCH)]
         ssd_all = [stats.tile([P, PACK], F32, name="ssd%d" % b, tag="ssd") for b in range(BATCH)]
+        std_all = [stats.tile([P, PACK], F32, name="std%d" % b, tag="std") for b in range(BATCH)]
         rstd_all = [stats.tile([P, PACK], F32, name="rstd%d" % b, tag="rstd") for b in range(BATCH)]
         xn_all = {}
         packed = {}
         banks = {}
         sums_all = {}
+        corrections = {}
 
         def mean_of(b):
             for t in range(PACK):
@@ -87,7 +89,7 @@ def tile_adaattn_pa_kernel(tc, c_1x, f_w, f_b, out):
                     bias=x_all[b][:, t, 0:1], accum_out=ssd_all[b][:, t : t + 1],
                 )
 
-        def rstd_of(b):
+        def correction_of(b):
             shift = stats.tile([P, PACK], F32)
             nc.gpsimd.tensor_tensor(
                 out=shift[:], in0=mean_all[b][:], in1=x_all[b][:, :, 0], op=ALU.subtract
@@ -99,14 +101,17 @@ def tile_adaattn_pa_kernel(tc, c_1x, f_w, f_b, out):
                 out=correction[:], in0=shift_sq[:], scalar1=-PIXELS / (PIXELS - 1), scalar2=EPS,
                 op0=ALU.mult, op1=ALU.add,
             )
-            scaled = stats.tile([P, PACK], F32)
-            nc.gpsimd.tensor_scalar(
-                out=scaled[:], in0=ssd_all[b][:], scalar1=1.0 / (PIXELS - 1), scalar2=0.0,
-                op0=ALU.mult, op1=ALU.add,
-            )
-            var = stats.tile([P, PACK], F32)
-            nc.gpsimd.tensor_tensor(out=var[:], in0=scaled[:], in1=correction[:], op=ALU.add)
-            nc.gpsimd.tensor_tensor(out=rstd_all[b][:], in0=var[:], in1=minus_half[:], op=ALU.pow)
+            corrections[b] = correction
+
+        def std_of(b):
+            for t in range(PACK):
+                nc.scalar.activation(
+                    out=std_all[b][:, t : t + 1], in_=ssd_all[b][:, t : t + 1], func=ACT.Sqrt,
+                    scale=1.0 / (PIXELS - 1), bias=corrections[b][:, t : t + 1],
+                )
+
+        def rstd_of(b):
+            nc.vector.reciprocal(out=rstd_all[b][:], in_=std_all[b][:])
 
         def normalise(b):
             xn = work.tile([P, PACK, PIXELS], BF16)
@@ -157,10 +162,10 @@ def tile_adaattn_pa_kernel(tc, c_1x, f_w, f_b, out):
                 first = h * HALF + m * M_TILE
                 nc.sync.dma_start(out=out[b, first : first + M_TILE, :], in_=o_sb[:])
 
-        minus_half = const.tile([P, PACK], F32)
-        nc.gpsimd.memset(minus_half[:], -0.5)
+        ones = const.tile([P, 1], F32)
+        nc.gpsimd.memset(ones[:], 1.0)
         table_junk = const.tile([P, 1], F32)
-        nc.scalar.activation(out=table_junk[:], in_=minus_half[:, 0:1], func=ACT.Square)
+        nc.scalar.activation(out=table_junk[:], in_=ones[:], func=ACT.Sqrt)
         ident = const.tile([P, P], F32)
         make_identity(nc, ident[:])
         ident_mean = const.tile([P, P], BF16)
@@ -182,11 +187,13 @@ def tile_adaattn_pa_kernel(tc, c_1x, f_w, f_b, out):
         nc.sync.dma_start(out=x_all[3][:], in_=x_dram[3])
 
         mean_of(0)
+        correction_of(0)
         squares_of(0, range(PACK))
-        rstd_of(0)
+        std_of(0)
         mean_of(1)
+        correction_of(1)
         squares_of(1, range(PACK))
-        rstd_of(1)
+        std_of(1)
 
         w_words = w_sb[:].bitcast(F32).rearrange("o a (q u) -> o a u q", u=2)
         w_grouped = const.tile([P, OUT_CH * PACK], BF16, align_bytes=64)
@@ -200,6 +207,8 @@ def tile_adaattn_pa_kernel(tc, c_1x, f_w, f_b, out):
                 out=w_grouped_words[:, 2 * pair : 2 * pair + 2, :, :],
                 in_=w_t[:].rearrange("q a u o -> q a o u"),
             )
+            if pair == 0:
+                rstd_of(0)
         w_codes = const.tile([P, OUT_CH], U32, align_bytes=64)
         w_scales = const.tile([P, OUT_CH], U8, align_bytes=64)
 
@@ -217,17 +226,26 @@ def tile_adaattn_pa_kernel(tc, c_1x, f_w, f_b, out):
         for b in range(BATCH):
             for h in range(HALVES):
                 step = b * HALVES + h
+                next_norm = h == HALVES - 1 and b + 1 < BATCH
                 if waiting is not None:
-                    add_bias_and_store(waiting[0], waiting[1], early)
-                if h == HALVES - 1 and b + 1 < BATCH:
+                    add_bias_and_store(waiting[0], waiting[1], early[:1])
+                    if next_norm:
+                        rstd_of(b + 1)
+                    add_bias_and_store(waiting[0], waiting[1], early[1:])
+                if next_norm:
                     normalise(b + 1)
                 quantise_and_multiply(b, h)
                 if step < len(sums_after):
                     partial_sums(3, sums_after[step])
                 if step == 0:
                     mean_from_sums(2)
+                    correction_of(2)
                 if step in squares_after:
                     squares_of(*squares_after[step])
+                    if step == 1:
+                        std_of(2)
+                    if step == 4:
+                        std_of(3)
                 if h == HALVES - 1:
                     if b + 1 < BATCH:
                         regroup_on_vector(b + 1, 0)
@@ -237,7 +255,6 @@ def tile_adaattn_pa_kernel(tc, c_1x, f_w, f_b, out):
                     add_bias_and_store(waiting[0], waiting[1], late)
                 if step == len(sums_after):
                     mean_from_sums(3)
-                if step in squares_after and squares_after[step][1][-1] == PACK - 1:
-                    rstd_of(squares_after[step][0])
+                    correction_of(3)
                 waiting = (b, h)
         add_bias_and_store(waiting[0], waiting[1], range(TILES_PER_HALF))

@@ -180,7 +180,7 @@ def tile_adaattn_pa_kernel(tc, c_1x, f_w, f_b, out):
             nc.sync.dma_start(out=x_all[0][:, t, :], in_=x_dram[0][:, t, :])
         for t in range(PACK):
             if t == PACK // 2:
-                nc.sync.dma_start(out=w_sb[:], in_=f_w.rearrange("(a o) c -> o a c", o=P))
+                nc.sync.dma_start(out=w_sb[:], in_=f_w.rearrange("(o a) c -> o a c", o=P))
             nc.sync.dma_start(out=x_all[1][:, t, :], in_=x_dram[1][:, t, :])
         nc.sync.dma_start(out=x_all[2][:], in_=x_dram[2])
         nc.sync.dma_start(out=bias[:], in_=f_b.partition_broadcast(P))
@@ -197,15 +197,15 @@ def tile_adaattn_pa_kernel(tc, c_1x, f_w, f_b, out):
 
         w_words = w_sb[:].bitcast(F32).rearrange("o a (q u) -> o a u q", u=2)
         w_grouped = const.tile([P, OUT_CH * PACK], BF16, align_bytes=64)
-        w_grouped_words = w_grouped[:].bitcast(F32).rearrange("q (a o u) -> q a o u", o=P, u=2)
+        w_grouped_words = w_grouped[:].bitcast(F32).rearrange("q (o k) -> q o k", o=P)
         for pair in range(2):
             w_t = psum.tile([P, 2, 2, P], F32, tag="bank")
             for a in range(2):
                 for u in range(2):
                     nc.tensor.transpose(w_t[:, a, u, :], w_words[:, 2 * pair + a, u, :], ident[:])
             nc.vector.tensor_copy(
-                out=w_grouped_words[:, 2 * pair : 2 * pair + 2, :, :],
-                in_=w_t[:].rearrange("q a u o -> q a o u"),
+                out=w_grouped_words[:, :, 4 * pair : 4 * pair + 4],
+                in_=w_t[:].rearrange("q a u o -> q o (a u)"),
             )
             if pair == 0:
                 rstd_of(0)
@@ -227,6 +227,9 @@ def tile_adaattn_pa_kernel(tc, c_1x, f_w, f_b, out):
             for h in range(HALVES):
                 step = b * HALVES + h
                 next_norm = h == HALVES - 1 and b + 1 < BATCH
+                if step == 1:
+                    mean_from_sums(2)
+                    correction_of(2)
                 if waiting is not None:
                     add_bias_and_store(waiting[0], waiting[1], early[:1])
                     if next_norm:
@@ -237,9 +240,6 @@ def tile_adaattn_pa_kernel(tc, c_1x, f_w, f_b, out):
                 quantise_and_multiply(b, h)
                 if step < len(sums_after):
                     partial_sums(3, sums_after[step])
-                if step == 0:
-                    mean_from_sums(2)
-                    correction_of(2)
                 if step in squares_after:
                     squares_of(*squares_after[step])
                     if step == 1:

@@ -24,7 +24,7 @@ HALVES = PIXELS // HALF
 M_TILE = P
 TILES_PER_HALF = HALF // M_TILE
 RUN = 4
-VECTOR_COLS = (256, 128, 0, 0)
+VECTOR_COLS = (320, 128, 0, 0)
 SUMMED = {2: (2, 3), 3: (0, 1, 2, 3)}
 CHUNKS = PIXELS // P
 
@@ -54,8 +54,8 @@ def tile_adaattn_pa_kernel(tc, c_1x, f_w, f_b, out):
         sums_all = {}
         corrections = {}
 
-        def mean_of(b):
-            for t in range(PACK):
+        def mean_of(b, slots=range(PACK)):
+            for t in slots:
                 if t in SUMMED.get(b, ()):
                     continue
                 v_junk = scratch.tile([P, PIXELS], BF16)
@@ -179,9 +179,8 @@ def tile_adaattn_pa_kernel(tc, c_1x, f_w, f_b, out):
         for t in range(PACK):
             nc.sync.dma_start(out=x_all[0][:, t, :], in_=x_dram[0][:, t, :])
         for t in range(PACK):
-            if t == PACK // 2:
-                nc.sync.dma_start(out=w_sb[:], in_=f_w.rearrange("(o a) c -> o a c", o=P))
             nc.sync.dma_start(out=x_all[1][:, t, :], in_=x_dram[1][:, t, :])
+        nc.sync.dma_start(out=w_sb[:], in_=f_w.rearrange("(o a) c -> o a c", o=P))
         nc.sync.dma_start(out=x_all[2][:], in_=x_dram[2])
         nc.sync.dma_start(out=bias[:], in_=f_b.partition_broadcast(P))
         nc.sync.dma_start(out=x_all[3][:], in_=x_dram[3])
@@ -190,7 +189,10 @@ def tile_adaattn_pa_kernel(tc, c_1x, f_w, f_b, out):
         correction_of(0)
         squares_of(0, range(PACK))
         std_of(0)
-        mean_of(1)
+        mean_of(1, range(PACK - 1))
+        rstd_of(0)
+        normalise(0)
+        mean_of(1, range(PACK - 1, PACK))
         correction_of(1)
         squares_of(1, range(PACK))
         std_of(1)
@@ -207,16 +209,13 @@ def tile_adaattn_pa_kernel(tc, c_1x, f_w, f_b, out):
                 out=w_grouped_words[:, :, 4 * pair : 4 * pair + 4],
                 in_=w_t[:].rearrange("q a u o -> q o (a u)"),
             )
-            if pair == 0:
-                rstd_of(0)
         w_codes = const.tile([P, OUT_CH], U32, align_bytes=64)
         w_scales = const.tile([P, OUT_CH], U8, align_bytes=64)
 
-        normalise(0)
+        regroup_on_vector(0, 0)
         nc.vector.quantize_mx(out=w_codes[:].bitcast(FP8X4), scales=w_scales[:], in_=w_grouped[:])
         partial_sums(2, SUMMED[2])
         mean_of(2)
-        regroup_on_vector(0, 0)
 
         early = range(TILES_PER_HALF // 2)
         late = range(TILES_PER_HALF // 2, TILES_PER_HALF)

@@ -26,8 +26,10 @@ TILES_PER_HALF = HALF // M_TILE
 RUN = 4
 VECTOR_COLS = (320, 128, 0, 0)
 SUMMED = {2: (2, 3), 3: (0, 1, 2, 3)}
-CHUNKS = PIXELS // P
+SUM_COLS = 32
+CHUNKS = PIXELS // SUM_COLS
 
+BN_SIZE = 6
 FLOPS = 2 * BATCH * PIXELS * CHANNELS * OUT_CH
 
 
@@ -52,7 +54,19 @@ def tile_adaattn_pa_kernel(tc, c_1x, f_w, f_b, out):
         packed = {}
         banks = {}
         sums_all = {}
+        one_pass = {}
         corrections = {}
+
+        def one_pass_parts(b, t):
+            parts = stats.tile([P, HALVES, BN_SIZE], F32)
+            for h in range(HALVES):
+                nc.vector.bn_stats(out=parts[:, h, :], in_=x_all[b][:, t, h * HALF : (h + 1) * HALF])
+            return parts
+
+        def one_pass_result(b, t, parts):
+            result = stats.tile([P, 2], F32)
+            nc.vector.bn_aggr(out=result[:], in_=parts[:])
+            one_pass[(b, t)] = result
 
         def mean_of(b, slots=range(PACK)):
             for t in slots:
@@ -66,12 +80,12 @@ def tile_adaattn_pa_kernel(tc, c_1x, f_w, f_b, out):
 
         def partial_sums(b, slots):
             if b not in sums_all:
-                sums_all[b] = psum_sums.tile([P, PACK, P], F32, name="sums%d" % b, tag="sums")
+                sums_all[b] = psum_sums.tile([P, PACK, SUM_COLS], F32, name="sums%d" % b, tag="sums")
             for t in slots:
                 for chunk in range(CHUNKS):
                     nc.tensor.matmul(
                         sums_all[b][:, t, :], lhsT=ident_mean[:],
-                        rhs=x_all[b][:, t, chunk * P : (chunk + 1) * P],
+                        rhs=x_all[b][:, t, chunk * SUM_COLS : (chunk + 1) * SUM_COLS],
                         start=chunk == 0, stop=chunk == CHUNKS - 1,
                     )
 
@@ -90,24 +104,29 @@ def tile_adaattn_pa_kernel(tc, c_1x, f_w, f_b, out):
                 )
 
         def correction_of(b):
+            n = PACK - 1 if b == 0 else PACK
             shift = stats.tile([P, PACK], F32)
             nc.gpsimd.tensor_tensor(
-                out=shift[:], in0=mean_all[b][:], in1=x_all[b][:, :, 0], op=ALU.subtract
+                out=shift[:, 0:n], in0=mean_all[b][:, 0:n], in1=x_all[b][:, 0:n, 0], op=ALU.subtract
             )
             shift_sq = stats.tile([P, PACK], F32)
-            nc.gpsimd.tensor_tensor(out=shift_sq[:], in0=shift[:], in1=shift[:], op=ALU.mult)
+            nc.gpsimd.tensor_tensor(out=shift_sq[:, 0:n], in0=shift[:, 0:n], in1=shift[:, 0:n], op=ALU.mult)
             correction = stats.tile([P, PACK], F32)
             nc.gpsimd.tensor_scalar(
-                out=correction[:], in0=shift_sq[:], scalar1=-PIXELS / (PIXELS - 1), scalar2=EPS,
+                out=correction[:, 0:n], in0=shift_sq[:, 0:n], scalar1=-PIXELS / (PIXELS - 1), scalar2=EPS,
                 op0=ALU.mult, op1=ALU.add,
             )
             corrections[b] = correction
 
         def std_of(b):
             for t in range(PACK):
+                if (b, t) in one_pass:
+                    squares, scale, offset = one_pass[(b, t)][:, 1:2], PIXELS / (PIXELS - 1), eps[:]
+                else:
+                    squares, scale = ssd_all[b][:, t : t + 1], 1.0 / (PIXELS - 1)
+                    offset = corrections[b][:, t : t + 1]
                 nc.scalar.activation(
-                    out=std_all[b][:, t : t + 1], in_=ssd_all[b][:, t : t + 1], func=ACT.Sqrt,
-                    scale=1.0 / (PIXELS - 1), bias=corrections[b][:, t : t + 1],
+                    out=std_all[b][:, t : t + 1], in_=squares, func=ACT.Sqrt, scale=scale, bias=offset,
                 )
 
         def rstd_of(b):
@@ -117,7 +136,7 @@ def tile_adaattn_pa_kernel(tc, c_1x, f_w, f_b, out):
             xn = work.tile([P, PACK, PIXELS], BF16)
             for t in range(PACK):
                 nc.vector.tensor_scalar(
-                    out=xn[:, t, :], in0=x_all[b][:, t, :], scalar1=mean_all[b][:, t : t + 1],
+                    out=xn[:, t, :], in0=x_all[b][:, t, :], scalar1=one_pass[(b, t)][:, 0:1] if (b, t) in one_pass else mean_all[b][:, t : t + 1],
                     scalar2=rstd_all[b][:, t : t + 1], op0=ALU.subtract, op1=ALU.mult,
                 )
             xn_all[b] = xn
@@ -164,6 +183,10 @@ def tile_adaattn_pa_kernel(tc, c_1x, f_w, f_b, out):
 
         ones = const.tile([P, 1], F32)
         nc.gpsimd.memset(ones[:], 1.0)
+        eps = const.tile([P, 1], F32)
+        nc.gpsimd.tensor_scalar(
+            out=eps[:], in0=ones[:], scalar1=0.0, scalar2=EPS, op0=ALU.mult, op1=ALU.add,
+        )
         table_junk = const.tile([P, 1], F32)
         nc.scalar.activation(out=table_junk[:], in_=ones[:], func=ACT.Sqrt)
         ident = const.tile([P, P], F32)
@@ -185,11 +208,14 @@ def tile_adaattn_pa_kernel(tc, c_1x, f_w, f_b, out):
         nc.sync.dma_start(out=bias[:], in_=f_b.partition_broadcast(P))
         nc.sync.dma_start(out=x_all[3][:], in_=x_dram[3])
 
-        mean_of(0)
+        mean_of(0, range(PACK - 1))
+        parts = one_pass_parts(0, PACK - 1)
         correction_of(0)
-        squares_of(0, range(PACK))
+        squares_of(0, range(PACK - 1))
+        mean_of(1, range(1))
+        one_pass_result(0, PACK - 1, parts)
         std_of(0)
-        mean_of(1, range(PACK - 1))
+        mean_of(1, range(1, PACK - 1))
         rstd_of(0)
         normalise(0)
         mean_of(1, range(PACK - 1, PACK))

from contextlib import ExitStack

import concourse.mybir as mybir
from concourse.masks import make_identity

BF16 = mybir.dt.bfloat16
F32 = mybir.dt.float32
U32 = mybir.dt.uint32
U8 = mybir.dt.uint8
FP8X4 = mybir.dt.float8_e4m3fn_x4
ALU = mybir.AluOpType
ACT = mybir.ActivationFunctionType
AXIS = mybir.AxisListType

P = 128
PACK = 4
BATCH = 4
CHANNELS = P * PACK
PIXELS = 1024
OUT_CH = 512
EPS = 1e-5
HALF = PIXELS // 2
HALVES = PIXELS // HALF
M_TILE = P
TILES_PER_HALF = HALF // M_TILE
RUN = 4
VECTOR_COLS = (320, 128, 0, 0)
SUMMED = {2: (2, 3), 3: (0, 1, 2, 3)}
SUM_COLS = 32
CHUNKS = PIXELS // SUM_COLS

BN_SIZE = 6
FLOPS = 2 * BATCH * PIXELS * CHANNELS * OUT_CH


def tile_adaattn_pa_kernel(tc, c_1x, f_w, f_b, out):
    nc = tc.nc
    with ExitStack() as stack:
        const = stack.enter_context(tc.tile_pool(name="const", bufs=1))
        stats = stack.enter_context(tc.tile_pool(name="stats", bufs=BATCH))
        scratch = stack.enter_context(tc.tile_pool(name="scratch", bufs=3))
        work = stack.enter_context(tc.tile_pool(name="work", bufs=2))
        results = stack.enter_context(tc.tile_pool(name="results", bufs=8))
        psum = stack.enter_context(tc.psum_pool(name="psum", bufs=7))
        psum_sums = stack.enter_context(tc.psum_pool(name="psum_sums", bufs=1))
        stack.enter_context(tc.manual_schedule())

        x_all = [const.tile([P, PACK, PIXELS], BF16, name="x%d" % b) for b in range(BATCH)]
        mean_all = [stats.tile([P, PACK], F32, name="mean%d" % b, tag="mean") for b in range(BATCH)]
        ssd_all = [stats.tile([P, PACK], F32, name="ssd%d" % b, tag="ssd") for b in range(BATCH)]
        std_all = [stats.tile([P, PACK], F32, name="std%d" % b, tag="std") for b in range(BATCH)]
        rstd_all = [stats.tile([P, PACK], F32, name="rstd%d" % b, tag="rstd") for b in range(BATCH)]
        xn_all = {}
        packed = {}
        banks = {}
        sums_all = {}
        one_pass = {}
        corrections = {}

        def one_pass_parts(b, t):
            parts = stats.tile([P, HALVES, BN_SIZE], F32)
            for h in range(HALVES):
                nc.vector.bn_stats(out=parts[:, h, :], in_=x_all[b][:, t, h * HALF : (h + 1) * HALF])
            return parts

        def one_pass_result(b, t, parts):
            result = stats.tile([P, 2], F32)
            nc.vector.bn_aggr(out=result[:], in_=parts[:])
            one_pass[(b, t)] = result

        def mean_of(b, slots=range(PACK)):
            for t in slots:
                if t in SUMMED.get(b, ()):
                    continue
                v_junk = scratch.tile([P, PIXELS], BF16)
                nc.vector.tensor_scalar(
                    out=v_junk[:], in0=x_all[b][:, t, :], scalar1=1.0 / PIXELS, scalar2=None,
                    op0=ALU.mult, op1=ALU.add, accum_out=mean_all[b][:, t : t + 1],
                )

        def partial_sums(b, slots):
            if b not in sums_all:
                sums_all[b] = psum_sums.tile([P, PACK, SUM_COLS], F32, name="sums%d" % b, tag="sums")
            for t in slots:
                for chunk in range(CHUNKS):
                    nc.tensor.matmul(
                        sums_all[b][:, t, :], lhsT=ident_mean[:],
                        rhs=x_all[b][:, t, chunk * SUM_COLS : (chunk + 1) * SUM_COLS],
                        start=chunk == 0, stop=chunk == CHUNKS - 1,
                    )

        def mean_from_sums(b):
            slots = slice(SUMMED[b][0], SUMMED[b][-1] + 1)
            nc.vector.tensor_reduce(
                out=mean_all[b][:, slots], in_=sums_all[b][:, slots, :], op=ALU.add, axis=AXIS.X
            )

        def squares_of(b, slots):
            for t in slots:
                s_junk = scratch.tile([P, PIXELS], BF16)
                nc.scalar.activation(
                    out=s_junk[:], in_=x_all[b][:, t, :], func=ACT.Square, scale=-1.0,
                    bias=x_all[b][:, t, 0:1], accum_out=ssd_all[b][:, t : t + 1],
                )

        def correction_of(b):
            n = PACK - 1 if b == 0 else PACK
            shift = stats.tile([P, PACK], F32)
            nc.gpsimd.tensor_tensor(
                out=shift[:, 0:n], in0=mean_all[b][:, 0:n], in1=x_all[b][:, 0:n, 0], op=ALU.subtract
            )
            shift_sq = stats.tile([P, PACK], F32)
            nc.gpsimd.tensor_tensor(out=shift_sq[:, 0:n], in0=shift[:, 0:n], in1=shift[:, 0:n], op=ALU.mult)
            correction = stats.tile([P, PACK], F32)
            nc.gpsimd.tensor_scalar(
                out=correction[:, 0:n], in0=shift_sq[:, 0:n], scalar1=-PIXELS / (PIXELS - 1), scalar2=EPS,
                op0=ALU.mult, op1=ALU.add,
            )
            corrections[b] = correction

        def std_of(b):
            for t in range(PACK):
                if (b, t) in one_pass:
                    squares, scale, offset = one_pass[(b, t)][:, 1:2], PIXELS / (PIXELS - 1), eps[:]
                else:
                    squares, scale = ssd_all[b][:, t : t + 1], 1.0 / (PIXELS - 1)
                    offset = corrections[b][:, t : t + 1]
                nc.scalar.activation(
                    out=std_all[b][:, t : t + 1], in_=squares, func=ACT.Sqrt, scale=scale, bias=offset,
                )

        def rstd_of(b):
            nc.vector.reciprocal(out=rstd_all[b][:], in_=std_all[b][:])

        def normalise(b):
            xn = work.tile([P, PACK, PIXELS], BF16)
            for t in range(PACK):
                nc.vector.tensor_scalar(
                    out=xn[:, t, :], in0=x_all[b][:, t, :], scalar1=one_pass[(b, t)][:, 0:1] if (b, t) in one_pass else mean_all[b][:, t : t + 1],
                    scalar2=rstd_all[b][:, t : t + 1], op0=ALU.subtract, op1=ALU.mult,
                )
            xn_all[b] = xn
            grouped = work.tile([P, PIXELS, PACK], BF16, align_bytes=64)
            codes = work.tile([P, PIXELS], U32, align_bytes=64)
            scales = work.tile([P, PIXELS], U8, align_bytes=64)
            packed[b] = (grouped, codes, scales)

        def regroup(copy, b, first, count):
            cols = slice(first, first + count)
            copy(
                out=packed[b][0][:, cols, :].rearrange("q (c i) t -> q c t i", i=RUN),
                in_=xn_all[b][:, :, cols].rearrange("q t (c i) -> q c t i", i=RUN),
            )

        def regroup_on_vector(b, h):
            if VECTOR_COLS[b] > 0:
                regroup(nc.vector.tensor_copy, b, (h + 1) * HALF - VECTOR_COLS[b], VECTOR_COLS[b])

        def quantise_and_multiply(b, h):
            regroup(nc.scalar.copy, b, h * HALF, HALF - VECTOR_COLS[b])
            grouped, codes, scales = packed[b]
            cols = slice(h * HALF, (h + 1) * HALF)
            nc.vector.quantize_mx(
                out=codes[:, cols].bitcast(FP8X4), scales=scales[:, cols],
                in_=grouped[:, cols, :].rearrange("q w t -> q (w t)"),
            )
            banks[(b, h)] = []
            for m in range(TILES_PER_HALF):
                m_cols = slice(h * HALF + m * M_TILE, h * HALF + (m + 1) * M_TILE)
                acc = psum.tile([M_TILE, OUT_CH], F32, tag="bank")
                nc.tensor.matmul_mx(
                    out=acc[:], lhsT=codes[:, m_cols].bitcast(FP8X4), lhsT_scale=scales[:, m_cols],
                    rhs=w_codes[:].bitcast(FP8X4), rhs_scale=w_scales[:], start=True, stop=True,
                )
                banks[(b, h)].append(acc)

        def add_bias_and_store(b, h, tiles):
            for m in tiles:
                o_sb = results.tile([M_TILE, OUT_CH], F32)
                nc.vector.tensor_tensor(out=o_sb[:], in0=banks[(b, h)][m][:], in1=bias[:], op=ALU.add)
                first = h * HALF + m * M_TILE
                nc.sync.dma_start(out=out[b, first : first + M_TILE, :], in_=o_sb[:])

        ones = const.tile([P, 1], F32)
        nc.gpsimd.memset(ones[:], 1.0)
        eps = const.tile([P, 1], F32)
        nc.gpsimd.tensor_scalar(
            out=eps[:], in0=ones[:], scalar1=0.0, scalar2=EPS, op0=ALU.mult, op1=ALU.add,
        )
        table_junk = const.tile([P, 1], F32)
        nc.scalar.activation(out=table_junk[:], in_=ones[:], func=ACT.Sqrt)
        ident = const.tile([P, P], F32)
        make_identity(nc, ident[:])
        ident_mean = const.tile([P, P], BF16)
        nc.gpsimd.tensor_scalar(
            out=ident_mean[:], in0=ident[:], scalar1=1.0 / PIXELS, scalar2=0.0,
            op0=ALU.mult, op1=ALU.add,
        )
        x_dram = [c_1x[b].rearrange("(q t) h w -> q t (h w)", t=PACK) for b in range(BATCH)]
        w_sb = const.tile([P, OUT_CH // P, CHANNELS], BF16)
        bias = const.tile([P, OUT_CH], BF16)
        for t in range(PACK):
            nc.sync.dma_start(out=x_all[0][:, t, :], in_=x_dram[0][:, t, :])
        for t in range(PACK):
            nc.sync.dma_start(out=x_all[1][:, t, :], in_=x_dram[1][:, t, :])
        nc.sync.dma_start(out=w_sb[:], in_=f_w.rearrange("(o a) c -> o a c", o=P))
        nc.sync.dma_start(out=x_all[2][:], in_=x_dram[2])
        nc.sync.dma_start(out=bias[:], in_=f_b.partition_broadcast(P))
        nc.sync.dma_start(out=x_all[3][:], in_=x_dram[3])

        mean_of(0, range(PACK - 1))
        parts = one_pass_parts(0, PACK - 1)
        correction_of(0)
        squares_of(0, range(PACK - 1))
        mean_of(1, range(1))
        one_pass_result(0, PACK - 1, parts)
        std_of(0)
        mean_of(1, range(1, PACK - 1))
        rstd_of(0)
        normalise(0)
        mean_of(1, range(PACK - 1, PACK))
        correction_of(1)
        squares_of(1, range(PACK))
        std_of(1)

        w_words = w_sb[:].bitcast(F32).rearrange("o a (q u) -> o a u q", u=2)
        w_grouped = const.tile([P, OUT_CH * PACK], BF16, align_bytes=64)
        w_grouped_words = w_grouped[:].bitcast(F32).rearrange("q (o k) -> q o k", o=P)
        for pair in range(2):
            w_t = psum.tile([P, 2, 2, P], F32, tag="bank")
            for a in range(2):
                for u in range(2):
                    nc.tensor.transpose(w_t[:, a, u, :], w_words[:, 2 * pair + a, u, :], ident[:])
            nc.vector.tensor_copy(
                out=w_grouped_words[:, :, 4 * pair : 4 * pair + 4],
                in_=w_t[:].rearrange("q a u o -> q o (a u)"),
            )
        w_codes = const.tile([P, OUT_CH], U32, align_bytes=64)
        w_scales = const.tile([P, OUT_CH], U8, align_bytes=64)

        regroup_on_vector(0, 0)
        nc.vector.quantize_mx(out=w_codes[:].bitcast(FP8X4), scales=w_scales[:], in_=w_grouped[:])
        partial_sums(2, SUMMED[2])
        mean_of(2)

        early = range(TILES_PER_HALF // 2)
        late = range(TILES_PER_HALF // 2, TILES_PER_HALF)
        waiting = None
        sums_after = [SUMMED[3][:2], SUMMED[3][2:3], SUMMED[3][3:]]
        squares_after = {1: (2, (0, 1, 2, 3)), 3: (3, (0, 1, 2)), 4: (3, (3,))}
        for b in range(BATCH):
            for h in range(HALVES):
                step = b * HALVES + h
                next_norm = h == HALVES - 1 and b + 1 < BATCH
                if step == 1:
                    mean_from_sums(2)
                    correction_of(2)
                if waiting is not None:
                    add_bias_and_store(waiting[0], waiting[1], early[:1])
                    if next_norm:
                        rstd_of(b + 1)
                    add_bias_and_store(waiting[0], waiting[1], early[1:])
                if next_norm:
                    normalise(b + 1)
                quantise_and_multiply(b, h)
                if step < len(sums_after):
                    partial_sums(3, sums_after[step])
                if step in squares_after:
                    squares_of(*squares_after[step])
                    if step == 1:
                        std_of(2)
                    if step == 4:
                        std_of(3)
                if h == HALVES - 1:
                    if b + 1 < BATCH:
                        regroup_on_vector(b + 1, 0)
                else:
                    regroup_on_vector(b, h + 1)
                if waiting is not None:
                    add_bias_and_store(waiting[0], waiting[1], late)
                if step == len(sums_after):
                    mean_from_sums(3)
                    correction_of(3)
                waiting = (b, h)
        add_bias_and_store(waiting[0], waiting[1], range(TILES_PER_HALF))
